import numpy as np
import ml_dtypes


def mxq(x, axis, fmt="e4m3"):
    dtype, down = {"e4m3": (ml_dtypes.float8_e4m3fn, 7), "e5m2": (ml_dtypes.float8_e5m2, 14)}[fmt]
    v = np.moveaxis(np.asarray(x, np.float32).astype(ml_dtypes.bfloat16).astype(np.float64), axis, -1)
    blocks = v.reshape(v.shape[:-1] + (-1, 32))
    amax = np.abs(blocks).max(-1, keepdims=True)
    byte = np.maximum(np.where(amax > 0, np.frexp(amax)[1] - 1 + 127, 0) - down, 1)
    scale = np.exp2(byte - 127.0)
    codes = (blocks / scale).astype(np.float32).astype(dtype).astype(np.float64)
    return np.moveaxis((codes * scale).reshape(v.shape), -1, axis)


WIDE = False


def mx_kscale(k):
    if not WIDE:
        return np.ones(k)
    levels = np.array([10, -10, 5, -5, 0])
    a = np.random.permutation(np.resize(levels, k // 512 * 4)).reshape(k // 512, 4)
    idx = np.arange(k)
    return np.exp2(a[idx // 512, idx % 128 // 32])


BF16 = ml_dtypes.bfloat16


def bf(x):
    return np.asarray(x, np.float32).astype(BF16)


def f64(x):
    return np.asarray(x).astype(np.float64)


B, I, C, K, L, S0, S1, S2, S3, S4 = 4, 32, 512, 7, 5, 16, 12, 8, 6, 4
P = S2 * S2


def setup_inputs():
    t = mx_kscale(C)
    return {"q": bf(np.random.standard_normal((B, I, C))),
            "feats": bf(np.random.standard_normal((B, C, S2, S2)) * t[:, None, None]),
            "po_w": bf(np.random.standard_normal((C, C)) / np.sqrt(C) / t),
            "po_b": bf(np.random.standard_normal(C) * 0.3)}


def reference(q, feats, po_w, po_b):
    m = f64(q)[:, :, :, None] * f64(feats).reshape(B, C, P)[:, None]
    o = (mxq(f64(po_w), 1, "e4m3") @ mxq(m, 2, "e4m3")) + f64(po_b)[:, None]
    return o.reshape(B, I, C, S2, S2)

@@ -1,0 +1,157 @@
+from contextlib import ExitStack
+
+import concourse.mybir as mybir
+from concourse.masks import make_identity
+
+BF16 = mybir.dt.bfloat16
+F32 = mybir.dt.float32
+U32 = mybir.dt.uint32
+U8 = mybir.dt.uint8
+FP8X4 = mybir.dt.float8_e4m3fn_x4
+
+P = 128
+PACK = 4
+HALF = 2
+IMAGES = 4
+INSTANCES = 32
+CHANNELS = 512
+POSITIONS = 64
+O_SUB = CHANNELS // P
+BANK = 512
+GROUP = BANK // POSITIONS
+GROUPS_PER_IMAGE = INSTANCES // GROUP
+STORE = 4
+
+FLOPS = 2 * IMAGES * INSTANCES * POSITIONS * CHANNELS * CHANNELS
+
+
+def tile_rpn_modulator_pb_kernel(tc, q, feats, po_w, po_b, out):
+    nc = tc.nc
+    with ExitStack() as ctx:
+        const = ctx.enter_context(tc.tile_pool(name="const", bufs=1))
+        work = ctx.enter_context(tc.tile_pool(name="work", bufs=3))
+        results = ctx.enter_context(tc.tile_pool(name="results", bufs=IMAGES * GROUPS_PER_IMAGE))
+        psum = ctx.enter_context(tc.psum_pool(name="psum", bufs=8))
+
+        q_rows = const.tile([P, CHANNELS], BF16)
+        nc.sync.dma_start(out=q_rows[:], in_=q.rearrange("b i c -> (b i) c"))
+        f_rows = const.tile([P, IMAGES, PACK, POSITIONS], BF16)
+        nc.scalar.dma_start(
+            out=f_rows[:].rearrange("k b t s -> k b (t s)"),
+            in_=feats.rearrange("b (k t) y x -> k b (t y x)", t=PACK),
+        )
+        w_rows = const.tile([P, O_SUB, CHANNELS], BF16)
+        w_dram = po_w.rearrange("(j r) c -> j r c", r=O_SUB)
+        for h in range(HALF):
+            two_r = slice(2 * h, 2 * h + 2)
+            nc.sync.dma_start(out=w_rows[:, two_r, :], in_=w_dram[:, two_r, :])
+        bias_bf = const.tile([P, O_SUB], BF16)
+        nc.scalar.dma_start(out=bias_bf[:], in_=po_b.rearrange("(j r) -> j r", r=O_SUB))
+
+        ident = const.tile([P, P], F32)
+        make_identity(nc, ident[:])
+
+        bias = const.tile([P, O_SUB], F32)
+        nc.vector.tensor_copy(out=bias[:], in_=bias_bf[:])
+
+        q_words = q_rows[:].bitcast(F32).rearrange("n (k u) -> n u k", u=HALF)
+        q_bank = psum.tile([P, BANK], F32, tag="bank")
+        for u in range(HALF):
+            nc.tensor.transpose(q_bank[:, u * P : (u + 1) * P], q_words[:, u, :], ident[:])
+        q_t = const.tile([P, IMAGES * INSTANCES, PACK], BF16)
+        nc.vector.tensor_copy(
+            out=q_t[:].bitcast(F32),
+            in_=q_bank[:, 0 : HALF * P].rearrange("k (u n) -> k n u", u=HALF),
+        )
+
+        f_t = const.tile([P, IMAGES, POSITIONS, PACK], BF16)
+        nc.vector.tensor_copy(out=f_t[:], in_=f_rows[:].rearrange("k b t s -> k b s t"))
+
+        w_t = const.tile([P, O_SUB, P, PACK], BF16, align_bytes=64)
+        w_codes = const.tile([P, O_SUB * P], U32, align_bytes=64)
+        w_scales = const.tile([P, O_SUB * P], U8, align_bytes=64)
+        w_words = w_rows[:].bitcast(F32).rearrange("j r (k u) -> j r u k", u=HALF)
+        for h in range(HALF):
+            two_r = slice(2 * h, 2 * h + 2)
+            w_bank = psum.tile([P, BANK], F32, tag="bank")
+            for rr in range(2):
+                for u in range(HALF):
+                    col = (rr * HALF + u) * P
+                    nc.tensor.transpose(
+                        w_bank[:, col : col + P], w_words[:, 2 * h + rr, u, :], ident[:]
+                    )
+            nc.scalar.copy(
+                out=w_t[:, two_r].bitcast(F32),
+                in_=w_bank[:].rearrange("k (r u j) -> k r j u", r=2, u=HALF),
+            )
+            cols = slice(2 * h * P, (2 * h + 2) * P)
+            nc.vector.quantize_mx(
+                out=w_codes[:, cols].bitcast(FP8X4),
+                scales=w_scales[:, cols],
+                in_=w_t[:, two_r].rearrange("k r j t -> k (r j t)"),
+            )
+
+        def quantise_m(g):
+            b = g // GROUPS_PER_IMAGE
+            shape = [P, GROUP, POSITIONS, PACK]
+            m_bf = work.tile(shape, BF16, align_bytes=64)
+            nc.vector.tensor_tensor(
+                out=m_bf[:],
+                in0=f_t[:, b].unsqueeze(1).to_broadcast(shape),
+                in1=q_t[:, g * GROUP : (g + 1) * GROUP, :].unsqueeze(2).to_broadcast(shape),
+                op=mybir.AluOpType.mult,
+            )
+            m_codes = work.tile([P, BANK], U32, align_bytes=64)
+            m_scales = work.tile([P, BANK], U8, align_bytes=64)
+            nc.vector.quantize_mx(
+                out=m_codes[:].bitcast(FP8X4),
+                scales=m_scales[:],
+                in_=m_bf[:].rearrange("k i s t -> k (i s t)"),
+            )
+            return m_codes, m_scales
+
+        def multiply_and_store(g, m_codes, m_scales):
+            b = g // GROUPS_PER_IMAGE
+            first = (g % GROUPS_PER_IMAGE) * GROUP
+            o_sb = results.tile([P, GROUP, O_SUB, POSITIONS], F32)
+            for r in range(O_SUB):
+                acc = psum.tile([P, BANK], F32, tag="bank")
+                nc.tensor.matmul_mx(
+                    out=acc[:],
+                    lhsT=w_codes[:, r * P : (r + 1) * P].bitcast(FP8X4),
+                    lhsT_scale=w_scales[:, r * P : (r + 1) * P],
+                    rhs=m_codes[:].bitcast(FP8X4),
+                    rhs_scale=m_scales[:],
+                    start=True,
+                    stop=True,
+                )
+                acc_view = acc[:].rearrange("j (i s) -> j i s", s=POSITIONS)
+                if r == O_SUB - 1:
+                    nc.vector.tensor_scalar(
+                        out=o_sb[:, :, r, :],
+                        in0=acc_view,
+                        scalar1=bias[:, r : r + 1],
+                        scalar2=None,
+                        op0=mybir.AluOpType.add,
+                    )
+                else:
+                    nc.scalar.activation(
+                        out=o_sb[:, :, r, :],
+                        in_=acc_view,
+                        func=mybir.ActivationFunctionType.Identity,
+                        bias=bias[:, r : r + 1],
+                        scale=1.0,
+                    )
+            out_rows = out[b].rearrange("i (j r) y x -> j i (r y x)", r=O_SUB)
+            for i0 in range(0, GROUP, STORE):
+                nc.sync.dma_start(
+                    out=out_rows[:, first + i0 : first + i0 + STORE, :],
+                    in_=o_sb[:, i0 : i0 + STORE].rearrange("j i r s -> j i (r s)"),
+                )
+
+        groups = IMAGES * GROUPS_PER_IMAGE
+        ready = quantise_m(0)
+        for g in range(groups):
+            following = quantise_m(g + 1) if g + 1 < groups else None
+            multiply_and_store(g, ready[0], ready[1])
+            ready = following

@@ -20,7 +20,7 @@ O_SUB = CHANNELS // P
 BANK = 512
 GROUP = BANK // POSITIONS
 GROUPS_PER_IMAGE = INSTANCES // GROUP
-STORE = 4
+STORE = 1
 
 FLOPS = 2 * IMAGES * INSTANCES * POSITIONS * CHANNELS * CHANNELS
 

@@ -17,10 +17,12 @@ INSTANCES = 32
 CHANNELS = 512
 POSITIONS = 64
 O_SUB = CHANNELS // P
-BANK = 512
-GROUP = BANK // POSITIONS
+GROUP = 4
+COLUMNS = GROUP * POSITIONS
 GROUPS_PER_IMAGE = INSTANCES // GROUP
-STORE = 1
+GROUPS = IMAGES * GROUPS_PER_IMAGE
+PSUM_BANKS = 8
+VECTOR_EVERY = 8
 
 FLOPS = 2 * IMAGES * INSTANCES * POSITIONS * CHANNELS * CHANNELS
 
@@ -30,66 +32,37 @@ def tile_rpn_modulator_pb_kernel(tc, q, feats, po_w, po_b, out):
     with ExitStack() as ctx:
         const = ctx.enter_context(tc.tile_pool(name="const", bufs=1))
         work = ctx.enter_context(tc.tile_pool(name="work", bufs=3))
-        results = ctx.enter_context(tc.tile_pool(name="results", bufs=IMAGES * GROUPS_PER_IMAGE))
-        psum = ctx.enter_context(tc.psum_pool(name="psum", bufs=8))
+        results = ctx.enter_context(tc.tile_pool(name="results", bufs=GROUPS))
+        psum = ctx.enter_context(tc.psum_pool(name="psum", bufs=PSUM_BANKS))
 
         q_rows = const.tile([P, CHANNELS], BF16)
-        nc.sync.dma_start(out=q_rows[:], in_=q.rearrange("b i c -> (b i) c"))
+        nc.scalar.dma_start(out=q_rows[:], in_=q.rearrange("b i c -> (b i) c"))
         f_rows = const.tile([P, IMAGES, PACK, POSITIONS], BF16)
-        nc.scalar.dma_start(
-            out=f_rows[:].rearrange("k b t s -> k b (t s)"),
-            in_=feats.rearrange("b (k t) y x -> k b (t y x)", t=PACK),
-        )
+        f_dram = feats.rearrange("b (k t) y x -> k b (t y x)", t=PACK)
+        f_flat = f_rows[:].rearrange("k b t s -> k b (t s)")
+        nc.scalar.dma_start(out=f_flat[:, 0:1, :], in_=f_dram[:, 0:1, :])
         w_rows = const.tile([P, O_SUB, CHANNELS], BF16)
         w_dram = po_w.rearrange("(j r) c -> j r c", r=O_SUB)
-        for h in range(HALF):
-            two_r = slice(2 * h, 2 * h + 2)
-            nc.sync.dma_start(out=w_rows[:, two_r, :], in_=w_dram[:, two_r, :])
-        bias_bf = const.tile([P, O_SUB], BF16)
-        nc.scalar.dma_start(out=bias_bf[:], in_=po_b.rearrange("(j r) -> j r", r=O_SUB))
+        for r in range(O_SUB):
+            nc.sync.dma_start(out=w_rows[:, r, :], in_=w_dram[:, r, :])
+        bias = const.tile([P, O_SUB], BF16)
+        nc.scalar.dma_start(out=bias[:], in_=po_b.rearrange("(j r) -> j r", r=O_SUB))
+        nc.scalar.dma_start(out=f_flat[:, 1:IMAGES, :], in_=f_dram[:, 1:IMAGES, :])
 
         ident = const.tile([P, P], F32)
         make_identity(nc, ident[:])
 
-        bias = const.tile([P, O_SUB], F32)
-        nc.vector.tensor_copy(out=bias[:], in_=bias_bf[:])
-
         q_words = q_rows[:].bitcast(F32).rearrange("n (k u) -> n u k", u=HALF)
-        q_bank = psum.tile([P, BANK], F32, tag="bank")
+        q_bank = psum.tile([P, HALF, P], F32, tag="bank")
         for u in range(HALF):
-            nc.tensor.transpose(q_bank[:, u * P : (u + 1) * P], q_words[:, u, :], ident[:])
+            nc.tensor.transpose(q_bank[:, u, :], q_words[:, u, :], ident[:])
         q_t = const.tile([P, IMAGES * INSTANCES, PACK], BF16)
-        nc.vector.tensor_copy(
-            out=q_t[:].bitcast(F32),
-            in_=q_bank[:, 0 : HALF * P].rearrange("k (u n) -> k n u", u=HALF),
-        )
+        nc.scalar.copy(out=q_t[:].bitcast(F32), in_=q_bank[:].rearrange("k u n -> k n u"))
 
         f_t = const.tile([P, IMAGES, POSITIONS, PACK], BF16)
-        nc.vector.tensor_copy(out=f_t[:], in_=f_rows[:].rearrange("k b t s -> k b s t"))
 
-        w_t = const.tile([P, O_SUB, P, PACK], BF16, align_bytes=64)
-        w_codes = const.tile([P, O_SUB * P], U32, align_bytes=64)
-        w_scales = const.tile([P, O_SUB * P], U8, align_bytes=64)
-        w_words = w_rows[:].bitcast(F32).rearrange("j r (k u) -> j r u k", u=HALF)
-        for h in range(HALF):
-            two_r = slice(2 * h, 2 * h + 2)
-            w_bank = psum.tile([P, BANK], F32, tag="bank")
-            for rr in range(2):
-                for u in range(HALF):
-                    col = (rr * HALF + u) * P
-                    nc.tensor.transpose(
-                        w_bank[:, col : col + P], w_words[:, 2 * h + rr, u, :], ident[:]
-                    )
-            nc.scalar.copy(
-                out=w_t[:, two_r].bitcast(F32),
-                in_=w_bank[:].rearrange("k (r u j) -> k r j u", r=2, u=HALF),
-            )
-            cols = slice(2 * h * P, (2 * h + 2) * P)
-            nc.vector.quantize_mx(
-                out=w_codes[:, cols].bitcast(FP8X4),
-                scales=w_scales[:, cols],
-                in_=w_t[:, two_r].rearrange("k r j t -> k (r j t)"),
-            )
+        def regroup_image(b):
+            nc.vector.tensor_copy(out=f_t[:, b], in_=f_rows[:, b].rearrange("k t s -> k s t"))
 
         def quantise_m(g):
             b = g // GROUPS_PER_IMAGE
@@ -101,8 +74,8 @@ def tile_rpn_modulator_pb_kernel(tc, q, feats, po_w, po_b, out):
                 in1=q_t[:, g * GROUP : (g + 1) * GROUP, :].unsqueeze(2).to_broadcast(shape),
                 op=mybir.AluOpType.mult,
             )
-            m_codes = work.tile([P, BANK], U32, align_bytes=64)
-            m_scales = work.tile([P, BANK], U8, align_bytes=64)
+            m_codes = work.tile([P, COLUMNS], U32, align_bytes=64)
+            m_scales = work.tile([P, COLUMNS], U8, align_bytes=64)
             nc.vector.quantize_mx(
                 out=m_codes[:].bitcast(FP8X4),
                 scales=m_scales[:],
@@ -110,26 +83,43 @@ def tile_rpn_modulator_pb_kernel(tc, q, feats, po_w, po_b, out):
             )
             return m_codes, m_scales
 
+        regroup_image(0)
+        ready = quantise_m(0)
+
+        w_t = const.tile([P, O_SUB, P, PACK], BF16, align_bytes=64)
+        w_codes = const.tile([P, O_SUB, P], U32, align_bytes=64)
+        w_scales = const.tile([P, O_SUB, P], U8, align_bytes=64)
+        w_words = w_rows[:].bitcast(F32).rearrange("j r (k u) -> j r u k", u=HALF)
+        for r in range(O_SUB):
+            w_bank = psum.tile([P, HALF, P], F32, tag="bank")
+            for u in range(HALF):
+                nc.tensor.transpose(w_bank[:, u, :], w_words[:, r, u, :], ident[:])
+            nc.scalar.copy(out=w_t[:, r].bitcast(F32), in_=w_bank[:].rearrange("k u j -> k j u"))
+            nc.vector.quantize_mx(
+                out=w_codes[:, r, :].bitcast(FP8X4),
+                scales=w_scales[:, r, :],
+                in_=w_t[:, r].rearrange("k j t -> k (j t)"),
+            )
+
         def multiply_and_store(g, m_codes, m_scales):
             b = g // GROUPS_PER_IMAGE
             first = (g % GROUPS_PER_IMAGE) * GROUP
             o_sb = results.tile([P, GROUP, O_SUB, POSITIONS], F32)
             for r in range(O_SUB):
-                acc = psum.tile([P, BANK], F32, tag="bank")
+                acc = psum.tile([P, GROUP, POSITIONS], F32, tag="bank")
                 nc.tensor.matmul_mx(
-                    out=acc[:],
-                    lhsT=w_codes[:, r * P : (r + 1) * P].bitcast(FP8X4),
-                    lhsT_scale=w_scales[:, r * P : (r + 1) * P],
+                    out=acc[:].rearrange("j i s -> j (i s)"),
+                    lhsT=w_codes[:, r, :].bitcast(FP8X4),
+                    lhsT_scale=w_scales[:, r, :],
                     rhs=m_codes[:].bitcast(FP8X4),
                     rhs_scale=m_scales[:],
                     start=True,
                     stop=True,
                 )
-                acc_view = acc[:].rearrange("j (i s) -> j i s", s=POSITIONS)
-                if r == O_SUB - 1:
+                if (g * O_SUB + r) % VECTOR_EVERY == VECTOR_EVERY - 1:
                     nc.vector.tensor_scalar(
                         out=o_sb[:, :, r, :],
-                        in0=acc_view,
+                        in0=acc[:],
                         scalar1=bias[:, r : r + 1],
                         scalar2=None,
                         op0=mybir.AluOpType.add,
@@ -137,21 +127,19 @@ def tile_rpn_modulator_pb_kernel(tc, q, feats, po_w, po_b, out):
                 else:
                     nc.scalar.activation(
                         out=o_sb[:, :, r, :],
-                        in_=acc_view,
+                        in_=acc[:],
                         func=mybir.ActivationFunctionType.Identity,
                         bias=bias[:, r : r + 1],
                         scale=1.0,
                     )
-            out_rows = out[b].rearrange("i (j r) y x -> j i (r y x)", r=O_SUB)
-            for i0 in range(0, GROUP, STORE):
-                nc.sync.dma_start(
-                    out=out_rows[:, first + i0 : first + i0 + STORE, :],
-                    in_=o_sb[:, i0 : i0 + STORE].rearrange("j i r s -> j i (r s)"),
-                )
+            nc.sync.dma_start(
+                out=out[b, first : first + GROUP].rearrange("i (j r) y x -> j i (r y x)", r=O_SUB),
+                in_=o_sb[:].rearrange("j i r s -> j i (r s)"),
+            )
 
-        groups = IMAGES * GROUPS_PER_IMAGE
-        ready = quantise_m(0)
-        for g in range(groups):
-            following = quantise_m(g + 1) if g + 1 < groups else None
+        for g in range(GROUPS):
+            if g % GROUPS_PER_IMAGE == 0 and g + GROUPS_PER_IMAGE < GROUPS:
+                regroup_image(g // GROUPS_PER_IMAGE + 1)
+            following = quantise_m(g + 1) if g + 1 < GROUPS else None
             multiply_and_store(g, ready[0], ready[1])
             ready = following

@@ -5,6 +5,7 @@ from concourse.masks import make_identity
 
 BF16 = mybir.dt.bfloat16
 F32 = mybir.dt.float32
+I32 = mybir.dt.int32
 U32 = mybir.dt.uint32
 U8 = mybir.dt.uint8
 FP8X4 = mybir.dt.float8_e4m3fn_x4
@@ -16,13 +17,16 @@ IMAGES = 4
 INSTANCES = 32
 CHANNELS = 512
 POSITIONS = 64
-O_SUB = CHANNELS // P
-GROUP = 4
-COLUMNS = GROUP * POSITIONS
+PAIR = 2
+SIDE = P // PAIR
+O_RUN = CHANNELS // SIDE
+W_PARTS = CHANNELS // P
+GROUP_PAIRS = 4
+COLUMNS = GROUP_PAIRS * POSITIONS
+GROUP = GROUP_PAIRS * PAIR
 GROUPS_PER_IMAGE = INSTANCES // GROUP
 GROUPS = IMAGES * GROUPS_PER_IMAGE
 PSUM_BANKS = 8
-VECTOR_EVERY = 8
 
 FLOPS = 2 * IMAGES * INSTANCES * POSITIONS * CHANNELS * CHANNELS
 
@@ -31,7 +35,7 @@ def tile_rpn_modulator_pb_kernel(tc, q, feats, po_w, po_b, out):
     nc = tc.nc
     with ExitStack() as ctx:
         const = ctx.enter_context(tc.tile_pool(name="const", bufs=1))
-        work = ctx.enter_context(tc.tile_pool(name="work", bufs=3))
+        work = ctx.enter_context(tc.tile_pool(name="work", bufs=6))
         results = ctx.enter_context(tc.tile_pool(name="results", bufs=GROUPS))
         psum = ctx.enter_context(tc.psum_pool(name="psum", bufs=PSUM_BANKS))
 
@@ -41,16 +45,24 @@ def tile_rpn_modulator_pb_kernel(tc, q, feats, po_w, po_b, out):
         f_dram = feats.rearrange("b (k t) y x -> k b (t y x)", t=PACK)
         f_flat = f_rows[:].rearrange("k b t s -> k b (t s)")
         nc.scalar.dma_start(out=f_flat[:, 0:1, :], in_=f_dram[:, 0:1, :])
-        w_rows = const.tile([P, O_SUB, CHANNELS], BF16)
-        w_dram = po_w.rearrange("(j r) c -> j r c", r=O_SUB)
-        for r in range(O_SUB):
+        w_rows = const.tile([P, W_PARTS, CHANNELS], BF16)
+        w_dram = po_w.rearrange("(j r) c -> j r c", r=W_PARTS)
+        for r in range(W_PARTS):
             nc.sync.dma_start(out=w_rows[:, r, :], in_=w_dram[:, r, :])
-        bias = const.tile([P, O_SUB], BF16)
-        nc.scalar.dma_start(out=bias[:], in_=po_b.rearrange("(j r) -> j r", r=O_SUB))
+        bias = const.tile([P, O_RUN], BF16)
+        for h in range(PAIR):
+            nc.scalar.dma_start(
+                out=bias[h * SIDE : (h + 1) * SIDE, :], in_=po_b.rearrange("(pp a) -> pp a", a=O_RUN)
+            )
         nc.scalar.dma_start(out=f_flat[:, 1:IMAGES, :], in_=f_dram[:, 1:IMAGES, :])
 
         ident = const.tile([P, P], F32)
         make_identity(nc, ident[:])
+
+        w_codes = const.tile([P, O_RUN, 3 * SIDE], U32, align_bytes=64)
+        w_scales = const.tile([P, O_RUN, 3 * SIDE], U8, align_bytes=64)
+        nc.vector.memset(w_codes[:].bitcast(I32), 0)
+        nc.vector.memset(w_scales[:].bitcast(I32), 0)
 
         q_words = q_rows[:].bitcast(F32).rearrange("n (k u) -> n u k", u=HALF)
         q_bank = psum.tile([P, HALF, P], F32, tag="bank")
@@ -66,80 +78,90 @@ def tile_rpn_modulator_pb_kernel(tc, q, feats, po_w, po_b, out):
 
         def quantise_m(g):
             b = g // GROUPS_PER_IMAGE
-            shape = [P, GROUP, POSITIONS, PACK]
-            m_bf = work.tile(shape, BF16, align_bytes=64)
-            nc.vector.tensor_tensor(
-                out=m_bf[:],
-                in0=f_t[:, b].unsqueeze(1).to_broadcast(shape),
-                in1=q_t[:, g * GROUP : (g + 1) * GROUP, :].unsqueeze(2).to_broadcast(shape),
-                op=mybir.AluOpType.mult,
-            )
-            m_codes = work.tile([P, COLUMNS], U32, align_bytes=64)
-            m_scales = work.tile([P, COLUMNS], U8, align_bytes=64)
-            nc.vector.quantize_mx(
-                out=m_codes[:].bitcast(FP8X4),
-                scales=m_scales[:],
-                in_=m_bf[:].rearrange("k i s t -> k (i s t)"),
-            )
-            return m_codes, m_scales
+            shape = [P, GROUP_PAIRS, POSITIONS, PACK]
+            q_group = q_t[:, g * GROUP : (g + 1) * GROUP, :].rearrange("k (ii h) t -> k h ii t", h=PAIR)
+            operands = []
+            for h in range(PAIR):
+                m_bf = work.tile(shape, BF16, align_bytes=64)
+                nc.vector.tensor_tensor(
+                    out=m_bf[:],
+                    in0=f_t[:, b].unsqueeze(1).to_broadcast(shape),
+                    in1=q_group[:, h].unsqueeze(2).to_broadcast(shape),
+                    op=mybir.AluOpType.mult,
+                )
+                m_codes = work.tile([P, COLUMNS], U32, align_bytes=64)
+                m_scales = work.tile([P, COLUMNS], U8, align_bytes=64)
+                nc.vector.quantize_mx(
+                    out=m_codes[:].bitcast(FP8X4),
+                    scales=m_scales[:],
+                    in_=m_bf[:].rearrange("k ii s t -> k (ii s t)"),
+                )
+                operands.append((m_codes, m_scales))
+            return operands
 
         regroup_image(0)
         ready = quantise_m(0)
 
-        w_t = const.tile([P, O_SUB, P, PACK], BF16, align_bytes=64)
-        w_codes = const.tile([P, O_SUB, P], U32, align_bytes=64)
-        w_scales = const.tile([P, O_SUB, P], U8, align_bytes=64)
+        w_t = const.tile([P, PAIR, W_PARTS, SIDE, PACK], BF16, align_bytes=64)
         w_words = w_rows[:].bitcast(F32).rearrange("j r (k u) -> j r u k", u=HALF)
-        for r in range(O_SUB):
+        for r in range(W_PARTS):
             w_bank = psum.tile([P, HALF, P], F32, tag="bank")
             for u in range(HALF):
                 nc.tensor.transpose(w_bank[:, u, :], w_words[:, r, u, :], ident[:])
-            nc.scalar.copy(out=w_t[:, r].bitcast(F32), in_=w_bank[:].rearrange("k u j -> k j u"))
-            nc.vector.quantize_mx(
-                out=w_codes[:, r, :].bitcast(FP8X4),
-                scales=w_scales[:, r, :],
-                in_=w_t[:, r].rearrange("k j t -> k (j t)"),
+            nc.scalar.copy(
+                out=w_t[:, :, r].bitcast(F32),
+                in_=w_bank[:].rearrange("k u (pp e) -> k e pp u", e=PAIR),
             )
+            for e in range(PAIR):
+                a = W_PARTS * e + r
+                nc.vector.quantize_mx(
+                    out=w_codes[:, a, SIDE : 2 * SIDE].bitcast(FP8X4),
+                    scales=w_scales[:, a, SIDE : 2 * SIDE],
+                    in_=w_t[:, e, r].rearrange("k pp t -> k (pp t)"),
+                )
 
-        def multiply_and_store(g, m_codes, m_scales):
+        def multiply_and_store(g, operands):
             b = g // GROUPS_PER_IMAGE
             first = (g % GROUPS_PER_IMAGE) * GROUP
-            o_sb = results.tile([P, GROUP, O_SUB, POSITIONS], F32)
-            for r in range(O_SUB):
-                acc = psum.tile([P, GROUP, POSITIONS], F32, tag="bank")
-                nc.tensor.matmul_mx(
-                    out=acc[:].rearrange("j i s -> j (i s)"),
-                    lhsT=w_codes[:, r, :].bitcast(FP8X4),
-                    lhsT_scale=w_scales[:, r, :],
-                    rhs=m_codes[:].bitcast(FP8X4),
-                    rhs_scale=m_scales[:],
-                    start=True,
-                    stop=True,
-                )
-                if (g * O_SUB + r) % VECTOR_EVERY == VECTOR_EVERY - 1:
+            o_sb = results.tile([P, GROUP_PAIRS, O_RUN, POSITIONS], F32)
+            for a in range(O_RUN):
+                acc = psum.tile([P, GROUP_PAIRS, POSITIONS], F32, tag="bank")
+                for h in range(PAIR):
+                    w_cols = slice((1 - h) * SIDE, (1 - h) * SIDE + P)
+                    nc.tensor.matmul_mx(
+                        out=acc[:].rearrange("p ii s -> p (ii s)"),
+                        lhsT=w_codes[:, a, w_cols].bitcast(FP8X4),
+                        lhsT_scale=w_scales[:, a, w_cols],
+                        rhs=operands[h][0][:].bitcast(FP8X4),
+                        rhs_scale=operands[h][1][:],
+                        start=(h == 0),
+                        stop=(h == PAIR - 1),
+                    )
+                if a == O_RUN - 1:
                     nc.vector.tensor_scalar(
-                        out=o_sb[:, :, r, :],
+                        out=o_sb[:, :, a, :],
                         in0=acc[:],
-                        scalar1=bias[:, r : r + 1],
+                        scalar1=bias[:, a : a + 1],
                         scalar2=None,
                         op0=mybir.AluOpType.add,
                     )
                 else:
                     nc.scalar.activation(
-                        out=o_sb[:, :, r, :],
+                        out=o_sb[:, :, a, :],
                         in_=acc[:],
                         func=mybir.ActivationFunctionType.Identity,
-                        bias=bias[:, r : r + 1],
+                        bias=bias[:, a : a + 1],
                         scale=1.0,
                     )
+            pieces = out[b, first : first + GROUP].rearrange("i o y x -> (i o y x)")
             nc.sync.dma_start(
-                out=out[b, first : first + GROUP].rearrange("i (j r) y x -> j i (r y x)", r=O_SUB),
-                in_=o_sb[:].rearrange("j i r s -> j i (r s)"),
+                out=pieces.rearrange("(ii p e) -> p ii e", p=P, e=O_RUN * POSITIONS),
+                in_=o_sb[:].rearrange("p ii a s -> p ii (a s)"),
             )
 
         for g in range(GROUPS):
             if g % GROUPS_PER_IMAGE == 0 and g + GROUPS_PER_IMAGE < GROUPS:
                 regroup_image(g // GROUPS_PER_IMAGE + 1)
             following = quantise_m(g + 1) if g + 1 < GROUPS else None
-            multiply_and_store(g, ready[0], ready[1])
+            multiply_and_store(g, ready)
             ready = following

@@ -54,7 +54,7 @@ def tile_rpn_modulator_pb_kernel(tc, q, feats, po_w, po_b, out):
             nc.scalar.dma_start(
                 out=bias[h * SIDE : (h + 1) * SIDE, :], in_=po_b.rearrange("(pp a) -> pp a", a=O_RUN)
             )
-        nc.scalar.dma_start(out=f_flat[:, 1:IMAGES, :], in_=f_dram[:, 1:IMAGES, :])
+        nc.sync.dma_start(out=f_flat[:, 1:IMAGES, :], in_=f_dram[:, 1:IMAGES, :])
 
         ident = const.tile([P, P], F32)
         make_identity(nc, ident[:])
@@ -102,14 +102,14 @@ def tile_rpn_modulator_pb_kernel(tc, q, feats, po_w, po_b, out):
         regroup_image(0)
         ready = quantise_m(0)
 
-        w_t = const.tile([P, PAIR, W_PARTS, SIDE, PACK], BF16, align_bytes=64)
+        w_t = const.tile([P, W_PARTS, PAIR, SIDE, PACK], BF16, align_bytes=64)
         w_words = w_rows[:].bitcast(F32).rearrange("j r (k u) -> j r u k", u=HALF)
         for r in range(W_PARTS):
             w_bank = psum.tile([P, HALF, P], F32, tag="bank")
             for u in range(HALF):
                 nc.tensor.transpose(w_bank[:, u, :], w_words[:, r, u, :], ident[:])
             nc.scalar.copy(
-                out=w_t[:, :, r].bitcast(F32),
+                out=w_t[:, r].bitcast(F32),
                 in_=w_bank[:].rearrange("k u (pp e) -> k e pp u", e=PAIR),
             )
             for e in range(PAIR):
@@ -117,7 +117,7 @@ def tile_rpn_modulator_pb_kernel(tc, q, feats, po_w, po_b, out):
                 nc.vector.quantize_mx(
                     out=w_codes[:, a, SIDE : 2 * SIDE].bitcast(FP8X4),
                     scales=w_scales[:, a, SIDE : 2 * SIDE],
-                    in_=w_t[:, e, r].rearrange("k pp t -> k (pp t)"),
+                    in_=w_t[:, r, e].rearrange("k pp t -> k (pp t)"),
                 )
 
         def multiply_and_store(g, operands):

@@ -27,6 +27,7 @@ GROUP = GROUP_PAIRS * PAIR
 GROUPS_PER_IMAGE = INSTANCES // GROUP
 GROUPS = IMAGES * GROUPS_PER_IMAGE
 PSUM_BANKS = 8
+STORE_CUTS = {0: (2, 4, 8), 1: (4, 8), 2: (4, 8), 3: (4, 8)}
 
 FLOPS = 2 * IMAGES * INSTANCES * POSITIONS * CHANNELS * CHANNELS
 
@@ -124,6 +125,10 @@ def tile_rpn_modulator_pb_kernel(tc, q, feats, po_w, po_b, out):
             b = g // GROUPS_PER_IMAGE
             first = (g % GROUPS_PER_IMAGE) * GROUP
             o_sb = results.tile([P, GROUP_PAIRS, O_RUN, POSITIONS], F32)
+            pieces = out[b, first : first + GROUP].rearrange("i o y x -> (i o y x)")
+            pieces = pieces.rearrange("(ii p e) -> p ii e", p=P, e=O_RUN * POSITIONS)
+            cuts = STORE_CUTS.get(g, (O_RUN,))
+            stored = 0
             for a in range(O_RUN):
                 acc = psum.tile([P, GROUP_PAIRS, POSITIONS], F32, tag="bank")
                 for h in range(PAIR):
@@ -153,11 +158,12 @@ def tile_rpn_modulator_pb_kernel(tc, q, feats, po_w, po_b, out):
                         bias=bias[:, a : a + 1],
                         scale=1.0,
                     )
-            pieces = out[b, first : first + GROUP].rearrange("i o y x -> (i o y x)")
-            nc.sync.dma_start(
-                out=pieces.rearrange("(ii p e) -> p ii e", p=P, e=O_RUN * POSITIONS),
-                in_=o_sb[:].rearrange("p ii a s -> p ii (a s)"),
-            )
+                if a + 1 in cuts:
+                    nc.sync.dma_start(
+                        out=pieces[:, :, stored * POSITIONS : (a + 1) * POSITIONS],
+                        in_=o_sb[:, :, stored : a + 1, :].rearrange("p ii a s -> p ii (a s)"),
+                    )
+                    stored = a + 1
 
         for g in range(GROUPS):
             if g % GROUPS_PER_IMAGE == 0 and g + GROUPS_PER_IMAGE < GROUPS:

@@ -17,17 +17,18 @@ IMAGES = 4
 INSTANCES = 32
 CHANNELS = 512
 POSITIONS = 64
+W_PARTS = CHANNELS // P
+PSUM_BANKS = 8
+PLAIN_SIZES = (4, 4, 8)
+PLAIN_INSTANCES = sum(PLAIN_SIZES)
 PAIR = 2
 SIDE = P // PAIR
 O_RUN = CHANNELS // SIDE
-W_PARTS = CHANNELS // P
 GROUP_PAIRS = 4
 COLUMNS = GROUP_PAIRS * POSITIONS
 GROUP = GROUP_PAIRS * PAIR
-GROUPS_PER_IMAGE = INSTANCES // GROUP
-GROUPS = IMAGES * GROUPS_PER_IMAGE
-PSUM_BANKS = 8
-STORE_CUTS = {0: (2, 4, 8), 1: (4, 8), 2: (4, 8), 3: (4, 8)}
+VECTOR_ROW = 3
+FIRST_CUTS = (4, 8)
 
 FLOPS = 2 * IMAGES * INSTANCES * POSITIONS * CHANNELS * CHANNELS
 
@@ -37,7 +38,7 @@ def tile_rpn_modulator_pb_kernel(tc, q, feats, po_w, po_b, out):
     with ExitStack() as ctx:
         const = ctx.enter_context(tc.tile_pool(name="const", bufs=1))
         work = ctx.enter_context(tc.tile_pool(name="work", bufs=6))
-        results = ctx.enter_context(tc.tile_pool(name="results", bufs=GROUPS))
+        results = ctx.enter_context(tc.tile_pool(name="results", bufs=1))
         psum = ctx.enter_context(tc.psum_pool(name="psum", bufs=PSUM_BANKS))
 
         q_rows = const.tile([P, CHANNELS], BF16)
@@ -50,9 +51,11 @@ def tile_rpn_modulator_pb_kernel(tc, q, feats, po_w, po_b, out):
         w_dram = po_w.rearrange("(j r) c -> j r c", r=W_PARTS)
         for r in range(W_PARTS):
             nc.sync.dma_start(out=w_rows[:, r, :], in_=w_dram[:, r, :])
+        plain_bias = const.tile([P, W_PARTS], BF16)
+        nc.scalar.dma_start(out=plain_bias[:], in_=po_b.rearrange("(j r) -> j r", r=W_PARTS))
         bias = const.tile([P, O_RUN], BF16)
         for h in range(PAIR):
-            nc.scalar.dma_start(
+            nc.sync.dma_start(
                 out=bias[h * SIDE : (h + 1) * SIDE, :], in_=po_b.rearrange("(pp a) -> pp a", a=O_RUN)
             )
         nc.sync.dma_start(out=f_flat[:, 1:IMAGES, :], in_=f_dram[:, 1:IMAGES, :])
@@ -77,41 +80,87 @@ def tile_rpn_modulator_pb_kernel(tc, q, feats, po_w, po_b, out):
         def regroup_image(b):
             nc.vector.tensor_copy(out=f_t[:, b], in_=f_rows[:, b].rearrange("k t s -> k s t"))
 
-        def quantise_m(g):
-            b = g // GROUPS_PER_IMAGE
-            shape = [P, GROUP_PAIRS, POSITIONS, PACK]
-            q_group = q_t[:, g * GROUP : (g + 1) * GROUP, :].rearrange("k (ii h) t -> k h ii t", h=PAIR)
-            operands = []
-            for h in range(PAIR):
-                m_bf = work.tile(shape, BF16, align_bytes=64)
-                nc.vector.tensor_tensor(
-                    out=m_bf[:],
-                    in0=f_t[:, b].unsqueeze(1).to_broadcast(shape),
-                    in1=q_group[:, h].unsqueeze(2).to_broadcast(shape),
-                    op=mybir.AluOpType.mult,
-                )
-                m_codes = work.tile([P, COLUMNS], U32, align_bytes=64)
-                m_scales = work.tile([P, COLUMNS], U8, align_bytes=64)
-                nc.vector.quantize_mx(
-                    out=m_codes[:].bitcast(FP8X4),
-                    scales=m_scales[:],
-                    in_=m_bf[:].rearrange("k ii s t -> k (ii s t)"),
-                )
-                operands.append((m_codes, m_scales))
-            return operands
+        def quantise_columns(b, q_columns, count):
+            shape = [P, count, POSITIONS, PACK]
+            m_bf = work.tile(shape, BF16, tag="m_bf", align_bytes=64)
+            nc.vector.tensor_tensor(
+                out=m_bf[:],
+                in0=f_t[:, b].unsqueeze(1).to_broadcast(shape),
+                in1=q_columns.unsqueeze(2).to_broadcast(shape),
+                op=mybir.AluOpType.mult,
+            )
+            m_codes = work.tile([P, count * POSITIONS], U32, tag="m_codes", align_bytes=64)
+            m_scales = work.tile([P, count * POSITIONS], U8, tag="m_scales", align_bytes=64)
+            nc.vector.quantize_mx(
+                out=m_codes[:].bitcast(FP8X4),
+                scales=m_scales[:],
+                in_=m_bf[:].rearrange("k i s t -> k (i s t)"),
+            )
+            return m_codes, m_scales
+
+        plain_groups = []
+        for size in PLAIN_SIZES:
+            plain_groups.append((sum(PLAIN_SIZES[: len(plain_groups)]), size))
+
+        def quantise_plain(n):
+            first, size = plain_groups[n]
+            return quantise_columns(0, q_t[:, first : first + size, :], size)
 
         regroup_image(0)
-        ready = quantise_m(0)
+        plain_ready = [quantise_plain(0)]
 
-        w_t = const.tile([P, W_PARTS, PAIR, SIDE, PACK], BF16, align_bytes=64)
+        w_plain = const.tile([P, W_PARTS, P, PACK], BF16, align_bytes=64)
+        plain_codes = const.tile([P, W_PARTS, P], U32, align_bytes=64)
+        plain_scales = const.tile([P, W_PARTS, P], U8, align_bytes=64)
         w_words = w_rows[:].bitcast(F32).rearrange("j r (k u) -> j r u k", u=HALF)
         for r in range(W_PARTS):
             w_bank = psum.tile([P, HALF, P], F32, tag="bank")
             for u in range(HALF):
                 nc.tensor.transpose(w_bank[:, u, :], w_words[:, r, u, :], ident[:])
+            nc.scalar.copy(out=w_plain[:, r].bitcast(F32), in_=w_bank[:].rearrange("k u j -> k j u"))
+            nc.vector.quantize_mx(
+                out=plain_codes[:, r, :].bitcast(FP8X4),
+                scales=plain_scales[:, r, :],
+                in_=w_plain[:, r].rearrange("k j t -> k (j t)"),
+            )
+
+        def multiply_plain(n):
+            first, size = plain_groups[n]
+            m_codes, m_scales = plain_ready[n]
+            o_sb = results.tile([P, size, W_PARTS, POSITIONS], F32, tag="plain%d" % n)
+            for r in range(W_PARTS):
+                acc = psum.tile([P, size, POSITIONS], F32, tag="bank")
+                nc.tensor.matmul_mx(
+                    out=acc[:].rearrange("p i s -> p (i s)"),
+                    lhsT=plain_codes[:, r, :].bitcast(FP8X4),
+                    lhsT_scale=plain_scales[:, r, :],
+                    rhs=m_codes[:].bitcast(FP8X4),
+                    rhs_scale=m_scales[:],
+                    start=True,
+                    stop=True,
+                )
+                nc.scalar.activation(
+                    out=o_sb[:, :, r, :],
+                    in_=acc[:],
+                    func=mybir.ActivationFunctionType.Identity,
+                    bias=plain_bias[:, r : r + 1],
+                    scale=1.0,
+                )
+            nc.sync.dma_start(
+                out=out[0, first : first + size].rearrange("i (j r) y x -> j i (r y x)", r=W_PARTS),
+                in_=o_sb[:].rearrange("j i r s -> j i (r s)"),
+            )
+
+        for n in range(len(PLAIN_SIZES)):
+            if n + 1 < len(PLAIN_SIZES):
+                plain_ready.append(quantise_plain(n + 1))
+            multiply_plain(n)
+
+        w_t = const.tile([P, W_PARTS, PAIR, SIDE, PACK], BF16, align_bytes=64)
+        for r in range(W_PARTS):
             nc.scalar.copy(
                 out=w_t[:, r].bitcast(F32),
-                in_=w_bank[:].rearrange("k u (pp e) -> k e pp u", e=PAIR),
+                in_=w_plain[:, r].bitcast(F32).rearrange("k (pp e) u -> k e pp u", e=PAIR),
             )
             for e in range(PAIR):
                 a = W_PARTS * e + r
@@ -121,13 +170,25 @@ def tile_rpn_modulator_pb_kernel(tc, q, feats, po_w, po_b, out):
                     in_=w_t[:, r, e].rearrange("k pp t -> k (pp t)"),
                 )
 
+        groups = []
+        for b in range(IMAGES):
+            for first in range(PLAIN_INSTANCES if b == 0 else 0, INSTANCES, GROUP):
+                groups.append((b, first))
+
+        def quantise_m(g):
+            b, first = groups[g]
+            if first == 0:
+                regroup_image(b)
+            n = b * INSTANCES + first
+            q_group = q_t[:, n : n + GROUP, :].rearrange("k (ii h) t -> k h ii t", h=PAIR)
+            return [quantise_columns(b, q_group[:, h], GROUP_PAIRS) for h in range(PAIR)]
+
         def multiply_and_store(g, operands):
-            b = g // GROUPS_PER_IMAGE
-            first = (g % GROUPS_PER_IMAGE) * GROUP
-            o_sb = results.tile([P, GROUP_PAIRS, O_RUN, POSITIONS], F32)
+            b, first = groups[g]
+            o_sb = results.tile([P, GROUP_PAIRS, O_RUN, POSITIONS], F32, tag="paired%d" % g)
             pieces = out[b, first : first + GROUP].rearrange("i o y x -> (i o y x)")
             pieces = pieces.rearrange("(ii p e) -> p ii e", p=P, e=O_RUN * POSITIONS)
-            cuts = STORE_CUTS.get(g, (O_RUN,))
+            cuts = FIRST_CUTS if g == 0 else (O_RUN,)
             stored = 0
             for a in range(O_RUN):
                 acc = psum.tile([P, GROUP_PAIRS, POSITIONS], F32, tag="bank")
@@ -142,7 +203,7 @@ def tile_rpn_modulator_pb_kernel(tc, q, feats, po_w, po_b, out):
                         start=(h == 0),
                         stop=(h == PAIR - 1),
                     )
-                if a == O_RUN - 1:
+                if a == VECTOR_ROW:
                     nc.vector.tensor_scalar(
                         out=o_sb[:, :, a, :],
                         in0=acc[:],
@@ -165,9 +226,8 @@ def tile_rpn_modulator_pb_kernel(tc, q, feats, po_w, po_b, out):
                     )
                     stored = a + 1
 
-        for g in range(GROUPS):
-            if g % GROUPS_PER_IMAGE == 0 and g + GROUPS_PER_IMAGE < GROUPS:
-                regroup_image(g // GROUPS_PER_IMAGE + 1)
-            following = quantise_m(g + 1) if g + 1 < GROUPS else None
+        ready = quantise_m(0)
+        for g in range(len(groups)):
+            following = quantise_m(g + 1) if g + 1 < len(groups) else None
             multiply_and_store(g, ready)
             ready = following

@@ -19,7 +19,7 @@ CHANNELS = 512
 POSITIONS = 64
 W_PARTS = CHANNELS // P
 PSUM_BANKS = 8
-PLAIN_SIZES = (4, 4, 8)
+PLAIN_SIZES = (4, 4, 4, 4)
 PLAIN_INSTANCES = sum(PLAIN_SIZES)
 PAIR = 2
 SIDE = P // PAIR

from contextlib import ExitStack

import concourse.mybir as mybir
from concourse.masks import make_identity

BF16 = mybir.dt.bfloat16
F32 = mybir.dt.float32
I32 = mybir.dt.int32
U32 = mybir.dt.uint32
U8 = mybir.dt.uint8
FP8X4 = mybir.dt.float8_e4m3fn_x4

P = 128
PACK = 4
HALF = 2
IMAGES = 4
INSTANCES = 32
CHANNELS = 512
POSITIONS = 64
W_PARTS = CHANNELS // P
PSUM_BANKS = 8
PLAIN_SIZES = (4, 4, 4, 4)
PLAIN_INSTANCES = sum(PLAIN_SIZES)
PAIR = 2
SIDE = P // PAIR
O_RUN = CHANNELS // SIDE
GROUP_PAIRS = 4
COLUMNS = GROUP_PAIRS * POSITIONS
GROUP = GROUP_PAIRS * PAIR
VECTOR_ROW = 3
FIRST_CUTS = (4, 8)

FLOPS = 2 * IMAGES * INSTANCES * POSITIONS * CHANNELS * CHANNELS


def tile_rpn_modulator_pb_kernel(tc, q, feats, po_w, po_b, out):
    nc = tc.nc
    with ExitStack() as ctx:
        const = ctx.enter_context(tc.tile_pool(name="const", bufs=1))
        work = ctx.enter_context(tc.tile_pool(name="work", bufs=6))
        results = ctx.enter_context(tc.tile_pool(name="results", bufs=1))
        psum = ctx.enter_context(tc.psum_pool(name="psum", bufs=PSUM_BANKS))

        q_rows = const.tile([P, CHANNELS], BF16)
        nc.scalar.dma_start(out=q_rows[:], in_=q.rearrange("b i c -> (b i) c"))
        f_rows = const.tile([P, IMAGES, PACK, POSITIONS], BF16)
        f_dram = feats.rearrange("b (k t) y x -> k b (t y x)", t=PACK)
        f_flat = f_rows[:].rearrange("k b t s -> k b (t s)")
        nc.scalar.dma_start(out=f_flat[:, 0:1, :], in_=f_dram[:, 0:1, :])
        w_rows = const.tile([P, W_PARTS, CHANNELS], BF16)
        w_dram = po_w.rearrange("(j r) c -> j r c", r=W_PARTS)
        for r in range(W_PARTS):
            nc.sync.dma_start(out=w_rows[:, r, :], in_=w_dram[:, r, :])
        plain_bias = const.tile([P, W_PARTS], BF16)
        nc.scalar.dma_start(out=plain_bias[:], in_=po_b.rearrange("(j r) -> j r", r=W_PARTS))
        bias = const.tile([P, O_RUN], BF16)
        for h in range(PAIR):
            nc.sync.dma_start(
                out=bias[h * SIDE : (h + 1) * SIDE, :], in_=po_b.rearrange("(pp a) -> pp a", a=O_RUN)
            )
        nc.sync.dma_start(out=f_flat[:, 1:IMAGES, :], in_=f_dram[:, 1:IMAGES, :])

        ident = const.tile([P, P], F32)
        make_identity(nc, ident[:])

        w_codes = const.tile([P, O_RUN, 3 * SIDE], U32, align_bytes=64)
        w_scales = const.tile([P, O_RUN, 3 * SIDE], U8, align_bytes=64)
        nc.vector.memset(w_codes[:].bitcast(I32), 0)
        nc.vector.memset(w_scales[:].bitcast(I32), 0)

        q_words = q_rows[:].bitcast(F32).rearrange("n (k u) -> n u k", u=HALF)
        q_bank = psum.tile([P, HALF, P], F32, tag="bank")
        for u in range(HALF):
            nc.tensor.transpose(q_bank[:, u, :], q_words[:, u, :], ident[:])
        q_t = const.tile([P, IMAGES * INSTANCES, PACK], BF16)
        nc.scalar.copy(out=q_t[:].bitcast(F32), in_=q_bank[:].rearrange("k u n -> k n u"))

        f_t = const.tile([P, IMAGES, POSITIONS, PACK], BF16)

        def regroup_image(b):
            nc.vector.tensor_copy(out=f_t[:, b], in_=f_rows[:, b].rearrange("k t s -> k s t"))

        def quantise_columns(b, q_columns, count):
            shape = [P, count, POSITIONS, PACK]
            m_bf = work.tile(shape, BF16, tag="m_bf", align_bytes=64)
            nc.vector.tensor_tensor(
                out=m_bf[:],
                in0=f_t[:, b].unsqueeze(1).to_broadcast(shape),
                in1=q_columns.unsqueeze(2).to_broadcast(shape),
                op=mybir.AluOpType.mult,
            )
            m_codes = work.tile([P, count * POSITIONS], U32, tag="m_codes", align_bytes=64)
            m_scales = work.tile([P, count * POSITIONS], U8, tag="m_scales", align_bytes=64)
            nc.vector.quantize_mx(
                out=m_codes[:].bitcast(FP8X4),
                scales=m_scales[:],
                in_=m_bf[:].rearrange("k i s t -> k (i s t)"),
            )
            return m_codes, m_scales

        plain_groups = []
        for size in PLAIN_SIZES:
            plain_groups.append((sum(PLAIN_SIZES[: len(plain_groups)]), size))

        def quantise_plain(n):
            first, size = plain_groups[n]
            return quantise_columns(0, q_t[:, first : first + size, :], size)

        regroup_image(0)
        plain_ready = [quantise_plain(0)]

        w_plain = const.tile([P, W_PARTS, P, PACK], BF16, align_bytes=64)
        plain_codes = const.tile([P, W_PARTS, P], U32, align_bytes=64)
        plain_scales = const.tile([P, W_PARTS, P], U8, align_bytes=64)
        w_words = w_rows[:].bitcast(F32).rearrange("j r (k u) -> j r u k", u=HALF)
        for r in range(W_PARTS):
            w_bank = psum.tile([P, HALF, P], F32, tag="bank")
            for u in range(HALF):
                nc.tensor.transpose(w_bank[:, u, :], w_words[:, r, u, :], ident[:])
            nc.scalar.copy(out=w_plain[:, r].bitcast(F32), in_=w_bank[:].rearrange("k u j -> k j u"))
            nc.vector.quantize_mx(
                out=plain_codes[:, r, :].bitcast(FP8X4),
                scales=plain_scales[:, r, :],
                in_=w_plain[:, r].rearrange("k j t -> k (j t)"),
            )

        def multiply_plain(n):
            first, size = plain_groups[n]
            m_codes, m_scales = plain_ready[n]
            o_sb = results.tile([P, size, W_PARTS, POSITIONS], F32, tag="plain%d" % n)
            for r in range(W_PARTS):
                acc = psum.tile([P, size, POSITIONS], F32, tag="bank")
                nc.tensor.matmul_mx(
                    out=acc[:].rearrange("p i s -> p (i s)"),
                    lhsT=plain_codes[:, r, :].bitcast(FP8X4),
                    lhsT_scale=plain_scales[:, r, :],
                    rhs=m_codes[:].bitcast(FP8X4),
                    rhs_scale=m_scales[:],
                    start=True,
                    stop=True,
                )
                nc.scalar.activation(
                    out=o_sb[:, :, r, :],
                    in_=acc[:],
                    func=mybir.ActivationFunctionType.Identity,
                    bias=plain_bias[:, r : r + 1],
                    scale=1.0,
                )
            nc.sync.dma_start(
                out=out[0, first : first + size].rearrange("i (j r) y x -> j i (r y x)", r=W_PARTS),
                in_=o_sb[:].rearrange("j i r s -> j i (r s)"),
            )

        for n in range(len(PLAIN_SIZES)):
            if n + 1 < len(PLAIN_SIZES):
                plain_ready.append(quantise_plain(n + 1))
            multiply_plain(n)

        w_t = const.tile([P, W_PARTS, PAIR, SIDE, PACK], BF16, align_bytes=64)
        for r in range(W_PARTS):
            nc.scalar.copy(
                out=w_t[:, r].bitcast(F32),
                in_=w_plain[:, r].bitcast(F32).rearrange("k (pp e) u -> k e pp u", e=PAIR),
            )
            for e in range(PAIR):
                a = W_PARTS * e + r
                nc.vector.quantize_mx(
                    out=w_codes[:, a, SIDE : 2 * SIDE].bitcast(FP8X4),
                    scales=w_scales[:, a, SIDE : 2 * SIDE],
                    in_=w_t[:, r, e].rearrange("k pp t -> k (pp t)"),
                )

        groups = []
        for b in range(IMAGES):
            for first in range(PLAIN_INSTANCES if b == 0 else 0, INSTANCES, GROUP):
                groups.append((b, first))

        def quantise_m(g):
            b, first = groups[g]
            if first == 0:
                regroup_image(b)
            n = b * INSTANCES + first
            q_group = q_t[:, n : n + GROUP, :].rearrange("k (ii h) t -> k h ii t", h=PAIR)
            return [quantise_columns(b, q_group[:, h], GROUP_PAIRS) for h in range(PAIR)]

        def multiply_and_store(g, operands):
            b, first = groups[g]
            o_sb = results.tile([P, GROUP_PAIRS, O_RUN, POSITIONS], F32, tag="paired%d" % g)
            pieces = out[b, first : first + GROUP].rearrange("i o y x -> (i o y x)")
            pieces = pieces.rearrange("(ii p e) -> p ii e", p=P, e=O_RUN * POSITIONS)
            cuts = FIRST_CUTS if g == 0 else (O_RUN,)
            stored = 0
            for a in range(O_RUN):
                acc = psum.tile([P, GROUP_PAIRS, POSITIONS], F32, tag="bank")
                for h in range(PAIR):
                    w_cols = slice((1 - h) * SIDE, (1 - h) * SIDE + P)
                    nc.tensor.matmul_mx(
                        out=acc[:].rearrange("p ii s -> p (ii s)"),
                        lhsT=w_codes[:, a, w_cols].bitcast(FP8X4),
                        lhsT_scale=w_scales[:, a, w_cols],
                        rhs=operands[h][0][:].bitcast(FP8X4),
                        rhs_scale=operands[h][1][:],
                        start=(h == 0),
                        stop=(h == PAIR - 1),
                    )
                if a == VECTOR_ROW:
                    nc.vector.tensor_scalar(
                        out=o_sb[:, :, a, :],
                        in0=acc[:],
                        scalar1=bias[:, a : a + 1],
                        scalar2=None,
                        op0=mybir.AluOpType.add,
                    )
                else:
                    nc.scalar.activation(
                        out=o_sb[:, :, a, :],
                        in_=acc[:],
                        func=mybir.ActivationFunctionType.Identity,
                        bias=bias[:, a : a + 1],
                        scale=1.0,
                    )
                if a + 1 in cuts:
                    nc.sync.dma_start(
                        out=pieces[:, :, stored * POSITIONS : (a + 1) * POSITIONS],
                        in_=o_sb[:, :, stored : a + 1, :].rearrange("p ii a s -> p ii (a s)"),
                    )
                    stored = a + 1

        ready = quantise_m(0)
        for g in range(len(groups)):
            following = quantise_m(g + 1) if g + 1 < len(groups) else None
            multiply_and_store(g, ready)
            ready = following
